import numpy as np
import ml_dtypes


def mxq(x, axis, fmt="e4m3"):
    dtype, down = {"e4m3": (ml_dtypes.float8_e4m3fn, 7), "e5m2": (ml_dtypes.float8_e5m2, 14)}[fmt]
    v = np.moveaxis(np.asarray(x, np.float32).astype(ml_dtypes.bfloat16).astype(np.float64), axis, -1)
    blocks = v.reshape(v.shape[:-1] + (-1, 32))
    amax = np.abs(blocks).max(-1, keepdims=True)
    byte = np.maximum(np.where(amax > 0, np.frexp(amax)[1] - 1 + 127, 0) - down, 1)
    scale = np.exp2(byte - 127.0)
    codes = (blocks / scale).astype(np.float32).astype(dtype).astype(np.float64)
    return np.moveaxis((codes * scale).reshape(v.shape), -1, axis)


WIDE = False


def mx_kscale(k):
    if not WIDE:
        return np.ones(k)
    levels = np.array([10, -10, 5, -5, 0])
    a = np.random.permutation(np.resize(levels, k // 512 * 4)).reshape(k // 512, 4)
    idx = np.arange(k)
    return np.exp2(a[idx // 512, idx % 128 // 32])


BF16 = ml_dtypes.bfloat16


def bf(x):
    return np.asarray(x, np.float32).astype(BF16)


def f64(x):
    return np.asarray(x).astype(np.float64)


E2M1 = np.array([0.0, 0.5, 1.0, 1.5, 2.0, 3.0, 4.0, 6.0, -0.0, -0.5, -1.0, -1.5, -2.0, -3.0, -4.0, -6.0])


def pack_weight(w, fmt):
    k, n = w.shape
    w = f64(bf(w)).reshape(k // 32, 32, n)
    amax = np.abs(w).max(1)
    if fmt == "e4m3":
        byte = np.frexp(amax)[1] - 1 + 127 - 7
    else:
        mant, ex = np.frexp(amax / 6.0)
        byte = np.where(mant > 0.5, ex, ex - 1) + 127
    byte = np.clip(np.where(amax > 0, byte, 1), 1, 254)
    scaled = (w * np.exp2(127.0 - byte)[:, None, :]).reshape(k, n).astype(np.float32)
    by_word = np.ascontiguousarray(scaled.reshape(k // 512, 128, 4, n).transpose(0, 1, 3, 2))
    if fmt == "e4m3":
        words = by_word.astype(ml_dtypes.float8_e4m3fn).view(np.uint8)
    else:
        c = by_word.astype(ml_dtypes.float4_e2m1fn).view(np.uint8) & 0xF
        words = c[..., 0::2] | (c[..., 1::2] << 4)
    return np.ascontiguousarray(words), np.ascontiguousarray(byte.astype(np.uint8).reshape(k // 512, 16, n))


def unpack_weight(words, scales, fmt):
    g, p, n, _ = words.shape
    if fmt == "e4m3":
        vals = np.ascontiguousarray(words).view(ml_dtypes.float8_e4m3fn).astype(np.float64)
    else:
        nib = np.empty((g, p, n, 4), np.uint8)
        nib[..., 0::2] = words & 0xF
        nib[..., 1::2] = words >> 4
        vals = E2M1[nib]
    vals = vals * np.repeat(np.exp2(scales.astype(np.float64) - 127.0), 8, axis=1)[..., None]
    return vals.transpose(0, 1, 3, 2).reshape(g * 512, n)


B, S, H, D, M = 2, 512, 16, 128, 1024
E = H * D
R = B * S
EPS = 1e-6


def setup_inputs():
    s = mx_kscale(E)
    query_input = bf(np.random.standard_normal((B, S, E)))
    norm_query_w = bf((1.0 + 0.1 * np.random.standard_normal(E)) * s)
    w_in = np.random.standard_normal((E, E)) / np.sqrt(E) / s[None, :]
    words, scales = pack_weight(np.ascontiguousarray(w_in.T), "e4m3")
    return {"query_input": query_input,
            "norm_query_w": norm_query_w,
            "W_in_words": words,
            "W_in_scales": scales}


def reference(query_input, norm_query_w, W_in_words, W_in_scales):
    x = f64(query_input).reshape(R, E)
    normed = x * (1.0 / np.sqrt(np.mean(x * x, 1, keepdims=True) + EPS))
    h = normed * f64(norm_query_w)
    return (mxq(h, 1, "e4m3") @ unpack_weight(W_in_words, W_in_scales, "e4m3")).reshape(B, S, E)

@@ -1,0 +1,172 @@
+from contextlib import ExitStack
+
+import concourse.mybir as mybir
+from concourse.masks import make_identity
+
+F32 = mybir.dt.float32
+BF16 = mybir.dt.bfloat16
+U8 = mybir.dt.uint8
+U32 = mybir.dt.uint32
+I32 = mybir.dt.int32
+FP8X4 = mybir.dt.float8_e4m3fn_x4
+ACT = mybir.ActivationFunctionType
+
+P = 128
+PACK = 4
+K_PASS = P * PACK
+ROWS = 1024
+FEATURES = 2048
+PASSES = FEATURES // K_PASS
+ROW_TILES = ROWS // P
+N_TILE = 512
+N_TILES = FEATURES // N_TILE
+SCALE_ROWS = 4
+QUADRANTS = 4
+EPS = 1e-6
+
+FLOPS = 2 * ROWS * FEATURES * FEATURES
+
+
+def tile_hopfieldmemorylayer_pa_kernel(tc, query_input, norm_query_w, W_in_words, W_in_scales, out):
+    nc = tc.nc
+    x_rows = query_input.flatten_outer_dims()
+    out_rows = out.flatten_outer_dims()
+
+    with ExitStack() as ctx:
+        keep = ctx.enter_context(tc.tile_pool(name="keep", bufs=1))
+        stats_pool = ctx.enter_context(tc.tile_pool(name="stats", bufs=4))
+        work = ctx.enter_context(tc.tile_pool(name="work", bufs=2))
+        results = ctx.enter_context(tc.tile_pool(name="results", bufs=3))
+        turned = ctx.enter_context(tc.psum_pool(name="turned", bufs=PASSES))
+        sums = ctx.enter_context(tc.psum_pool(name="sums", bufs=N_TILES))
+        ctx.enter_context(tc.manual_schedule())
+
+        x_all = keep.tile([P, ROW_TILES, FEATURES], BF16)
+        w_codes = keep.tile([P, PASSES, FEATURES], U32, align_bytes=64)
+        w_planes = keep.tile([P, FEATURES], U8, align_bytes=64)
+        gain_words = keep.tile([P, PASSES, PACK], BF16)
+        identity = keep.tile([P, P], F32)
+        eps = keep.tile([P, 1], F32)
+        table_warm = keep.tile([P, 1], F32)
+
+        def load_rows(i):
+            nc.sync.dma_start(out=x_all[:, i, :], in_=x_rows[i * P : (i + 1) * P, :])
+
+        def load_weight_scales():
+            nc.vector.memset(w_planes[:].bitcast(I32), 0)
+            for quadrant in range(QUADRANTS):
+                first = 32 * quadrant
+                nc.sync.dma_start(
+                    out=w_planes[first : first + PASSES * SCALE_ROWS, :].bitcast(I32),
+                    in_=W_in_scales[:, SCALE_ROWS * quadrant : SCALE_ROWS * (quadrant + 1), :].bitcast(I32),
+                )
+
+        def load_weight_columns(n):
+            words = W_in_words.rearrange("g p n t -> p g (n t)")
+            nc.sync.dma_start(
+                out=w_codes[:, :, n * N_TILE : (n + 1) * N_TILE].bitcast(I32),
+                in_=words[:, :, n * N_TILE * PACK : (n + 1) * N_TILE * PACK].bitcast(I32),
+            )
+
+        def statistics(i):
+            squares = work.tile([P, FEATURES], BF16)
+            sum_squares = stats_pool.tile([P, 1], F32)
+            nc.scalar.activation(out=squares[:], in_=x_all[:, i, :], func=ACT.Square, accum_out=sum_squares[:])
+            rms = stats_pool.tile([P, 1], F32)
+            nc.scalar.activation(out=rms[:], in_=sum_squares[:], func=ACT.Sqrt, scale=1.0 / FEATURES, bias=eps[:])
+            return rms
+
+        def normalise(i, rms):
+            inv_rms = stats_pool.tile([P, 1], F32)
+            nc.vector.reciprocal(inv_rms[:], rms[:])
+            y = work.tile([P, PASSES, PACK, P], F32)
+            nc.vector.tensor_scalar_mul(
+                out=y[:],
+                in0=x_all[:, i, :].rearrange("r (g p t) -> r g t p", p=P, t=PACK),
+                scalar1=inv_rms[:],
+            )
+            return y
+
+        def transpose(y):
+            banks = []
+            for g in range(PASSES):
+                y_turned = turned.tile([P, PACK, P], F32, name="y_turned")
+                for t in range(PACK):
+                    nc.tensor.transpose(y_turned[:, t, :], y[:, g, t, :], identity[:])
+                banks.append(y_turned)
+            return banks
+
+        def gain(banks):
+            h = work.tile([P, PASSES, P, PACK], BF16, align_bytes=64)
+            for g in range(PASSES):
+                nc.vector.tensor_tensor(
+                    out=h[:, g, :, :],
+                    in0=banks[g][:].rearrange("p t r -> p r t"),
+                    in1=gain_words[:, g, :].unsqueeze(1).to_broadcast([P, P, PACK]),
+                    op=mybir.AluOpType.mult,
+                )
+            return h
+
+        def quantise(h):
+            h_codes = work.tile([P, PASSES, P], U32, align_bytes=64)
+            h_planes = work.tile([P, PASSES, P], U8, align_bytes=64)
+            nc.vector.quantize_mx(
+                out=h_codes[:].rearrange("p g r -> p (g r)").bitcast(FP8X4),
+                scales=h_planes[:].rearrange("p g r -> p (g r)"),
+                in_=h[:].rearrange("p g r t -> p (g r t)"),
+            )
+            return h_codes, h_planes
+
+        def project(i, h_codes, h_planes):
+            result = results.tile([P, FEATURES], F32)
+            for n in range(N_TILES):
+                n_cols = slice(n * N_TILE, (n + 1) * N_TILE)
+                acc = sums.tile([P, N_TILE], F32)
+                for g in range(PASSES):
+                    nc.tensor.matmul_mx(
+                        out=acc[:],
+                        lhsT=h_codes[:, g, :].bitcast(FP8X4),
+                        lhsT_scale=h_planes[:, g, :],
+                        rhs=w_codes[:, g, n_cols].bitcast(FP8X4),
+                        rhs_scale=w_planes[SCALE_ROWS * g : P, n_cols],
+                        start=(g == 0),
+                        stop=(g == PASSES - 1),
+                    )
+                nc.scalar.copy(out=result[:, n_cols], in_=acc[:])
+                nc.sync.dma_start(out=out_rows[i * P : (i + 1) * P, n_cols], in_=result[:, n_cols])
+
+        with nc.allow_non_contiguous_dma(reason="the gain, four neighbouring features to a partition"):
+            nc.scalar.dma_start(out=gain_words[:], in_=norm_query_w.rearrange("(g p t) -> p g t", p=P, t=PACK))
+        nc.vector.memset(eps[:], EPS)
+        nc.scalar.activation(out=table_warm[:], in_=eps[:], func=ACT.Sqrt)
+        make_identity(nc, identity[:])
+
+        load_rows(0)
+        load_rows(1)
+        load_weight_scales()
+        load_weight_columns(0)
+        load_weight_columns(1)
+        load_rows(2)
+        load_weight_columns(2)
+        load_weight_columns(3)
+        for i in range(3, ROW_TILES):
+            load_rows(i)
+
+        rms = {0: statistics(0), 1: statistics(1)}
+        y = {0: normalise(0, rms[0])}
+        banks = transpose(y[0])
+        h = gain(banks)
+        y[1] = normalise(1, rms[1])
+        quantised = {0: quantise(h)}
+        for i in range(ROW_TILES):
+            if i + 1 < ROW_TILES:
+                banks = transpose(y[i + 1])
+            if i + 2 < ROW_TILES:
+                rms[i + 2] = statistics(i + 2)
+            if i + 1 < ROW_TILES:
+                h = gain(banks)
+            if i + 2 < ROW_TILES:
+                y[i + 2] = normalise(i + 2, rms[i + 2])
+            if i + 1 < ROW_TILES:
+                quantised[i + 1] = quantise(h)
+            project(i, quantised[i][0], quantised[i][1])

@@ -22,6 +22,7 @@ N_TILE = 512
 N_TILES = FEATURES // N_TILE
 SCALE_ROWS = 4
 QUADRANTS = 4
+LINE = 4
 EPS = 1e-6
 
 FLOPS = 2 * ROWS * FEATURES * FEATURES
@@ -80,11 +81,12 @@ def tile_hopfieldmemorylayer_pa_kernel(tc, query_input, norm_query_w, W_in_words
             inv_rms = stats_pool.tile([P, 1], F32)
             nc.vector.reciprocal(inv_rms[:], rms[:])
             y = work.tile([P, PASSES, PACK, P], F32)
-            nc.vector.tensor_scalar_mul(
-                out=y[:],
-                in0=x_all[:, i, :].rearrange("r (g p t) -> r g t p", p=P, t=PACK),
-                scalar1=inv_rms[:],
-            )
+            for g in range(PASSES):
+                nc.vector.tensor_scalar_mul(
+                    out=y[:, g, :, :].rearrange("r t (c j) -> r c t j", j=LINE),
+                    in0=x_all[:, i, g * K_PASS : (g + 1) * K_PASS].rearrange("r (c j t) -> r c t j", j=LINE, t=PACK),
+                    scalar1=inv_rms[:],
+                )
             return y
 
         def transpose(y):

@@ -10,9 +10,12 @@ U32 = mybir.dt.uint32
 I32 = mybir.dt.int32
 FP8X4 = mybir.dt.float8_e4m3fn_x4
 ACT = mybir.ActivationFunctionType
+ALU = mybir.AluOpType
 
 P = 128
 PACK = 4
+PAIR = 2
+HALVES = PACK // PAIR
 K_PASS = P * PACK
 ROWS = 1024
 FEATURES = 2048
@@ -22,7 +25,7 @@ N_TILE = 512
 N_TILES = FEATURES // N_TILE
 SCALE_ROWS = 4
 QUADRANTS = 4
-LINE = 4
+PASSES_A_BANK = 2
 EPS = 1e-6
 
 FLOPS = 2 * ROWS * FEATURES * FEATURES
@@ -38,14 +41,16 @@ def tile_hopfieldmemorylayer_pa_kernel(tc, query_input, norm_query_w, W_in_words
         stats_pool = ctx.enter_context(tc.tile_pool(name="stats", bufs=4))
         work = ctx.enter_context(tc.tile_pool(name="work", bufs=2))
         results = ctx.enter_context(tc.tile_pool(name="results", bufs=3))
-        turned = ctx.enter_context(tc.psum_pool(name="turned", bufs=PASSES))
+        turned = ctx.enter_context(tc.psum_pool(name="turned", bufs=4))
         sums = ctx.enter_context(tc.psum_pool(name="sums", bufs=N_TILES))
         ctx.enter_context(tc.manual_schedule())
 
         x_all = keep.tile([P, ROW_TILES, FEATURES], BF16)
         w_codes = keep.tile([P, PASSES, FEATURES], U32, align_bytes=64)
         w_planes = keep.tile([P, FEATURES], U8, align_bytes=64)
-        gain_words = keep.tile([P, PASSES, PACK], BF16)
+        gain_row = keep.tile([P, FEATURES], BF16)
+        gain_sorted = keep.tile([P, HALVES, PASSES, P, PAIR], BF16)
+        ones = keep.tile([P, P], BF16)
         identity = keep.tile([P, P], F32)
         eps = keep.tile([P, 1], F32)
         table_warm = keep.tile([P, 1], F32)
@@ -69,6 +74,15 @@ def tile_hopfieldmemorylayer_pa_kernel(tc, query_input, norm_query_w, W_in_words
                 in_=words[:, :, n * N_TILE * PACK : (n + 1) * N_TILE * PACK].bitcast(I32),
             )
 
+        def spread_gain():
+            for g in range(PASSES):
+                acc = sums.tile([P, N_TILE], F32, name="acc")
+                nc.tensor.matmul(out=acc[:], lhsT=ones[:], rhs=gain_row[:, g * K_PASS : (g + 1) * K_PASS], start=True, stop=True)
+                nc.vector.tensor_copy(
+                    out=gain_sorted[:, :, g, :, :],
+                    in_=acc[:].rearrange("r (p u e) -> r u p e", u=HALVES, e=PAIR),
+                )
+
         def statistics(i):
             squares = work.tile([P, FEATURES], BF16)
             sum_squares = stats_pool.tile([P, 1], F32)
@@ -80,32 +94,39 @@ def tile_hopfieldmemorylayer_pa_kernel(tc, query_input, norm_query_w, W_in_words
         def normalise(i, rms):
             inv_rms = stats_pool.tile([P, 1], F32)
             nc.vector.reciprocal(inv_rms[:], rms[:])
-            y = work.tile([P, PASSES, PACK, P], F32)
-            for g in range(PASSES):
-                nc.vector.tensor_scalar_mul(
-                    out=y[:, g, :, :].rearrange("r t (c j) -> r c t j", j=LINE),
-                    in0=x_all[:, i, g * K_PASS : (g + 1) * K_PASS].rearrange("r (c j t) -> r c t j", j=LINE, t=PACK),
-                    scalar1=inv_rms[:],
+            h_sorted = work.tile([P, HALVES, PASSES * P, PAIR], BF16)
+            pairs = x_all[:, i, :].rearrange("r (c u e) -> r u c e", u=HALVES, e=PAIR)
+            for u in range(HALVES):
+                nc.vector.scalar_tensor_tensor(
+                    out=h_sorted[:, u, :, :],
+                    in0=pairs[:, u, :, :],
+                    scalar=inv_rms[:],
+                    in1=gain_sorted[:, u, :, :, :].rearrange("r g p e -> r (g p) e"),
+                    op0=ALU.mult,
+                    op1=ALU.mult,
                 )
-            return y
+            return h_sorted
 
-        def transpose(y):
+        def transpose(h_sorted):
+            words = h_sorted[:].rearrange("r u c e -> r (u c e)").bitcast(F32)
             banks = []
-            for g in range(PASSES):
-                y_turned = turned.tile([P, PACK, P], F32, name="y_turned")
-                for t in range(PACK):
-                    nc.tensor.transpose(y_turned[:, t, :], y[:, g, t, :], identity[:])
-                banks.append(y_turned)
+            for b in range(PASSES // PASSES_A_BANK):
+                bank = turned.tile([P, PASSES_A_BANK, HALVES, P], F32, name="bank")
+                for j in range(PASSES_A_BANK):
+                    g = b * PASSES_A_BANK + j
+                    for u in range(HALVES):
+                        first = (u * PASSES + g) * P
+                        nc.tensor.transpose(bank[:, j, u, :], words[:, first : first + P], identity[:])
+                banks.append(bank)
             return banks
 
-        def gain(banks):
+        def gather(banks):
             h = work.tile([P, PASSES, P, PACK], BF16, align_bytes=64)
-            for g in range(PASSES):
-                nc.vector.tensor_tensor(
-                    out=h[:, g, :, :],
-                    in0=banks[g][:].rearrange("p t r -> p r t"),
-                    in1=gain_words[:, g, :].unsqueeze(1).to_broadcast([P, P, PACK]),
-                    op=mybir.AluOpType.mult,
+            h_words = h[:].rearrange("p g r t -> p (g r t)").bitcast(F32).rearrange("p (g r u) -> p g r u", g=PASSES, u=HALVES)
+            for b in range(PASSES // PASSES_A_BANK):
+                nc.vector.tensor_copy(
+                    out=h_words[:, b * PASSES_A_BANK : (b + 1) * PASSES_A_BANK, :, :],
+                    in_=banks[b][:].rearrange("p g u r -> p g r u"),
                 )
             return h
 
@@ -123,7 +144,7 @@ def tile_hopfieldmemorylayer_pa_kernel(tc, query_input, norm_query_w, W_in_words
             result = results.tile([P, FEATURES], F32)
             for n in range(N_TILES):
                 n_cols = slice(n * N_TILE, (n + 1) * N_TILE)
-                acc = sums.tile([P, N_TILE], F32)
+                acc = sums.tile([P, N_TILE], F32, name="acc")
                 for g in range(PASSES):
                     nc.tensor.matmul_mx(
                         out=acc[:],
@@ -137,8 +158,9 @@ def tile_hopfieldmemorylayer_pa_kernel(tc, query_input, norm_query_w, W_in_words
                 nc.scalar.copy(out=result[:, n_cols], in_=acc[:])
                 nc.sync.dma_start(out=out_rows[i * P : (i + 1) * P, n_cols], in_=result[:, n_cols])
 
-        with nc.allow_non_contiguous_dma(reason="the gain, four neighbouring features to a partition"):
-            nc.scalar.dma_start(out=gain_words[:], in_=norm_query_w.rearrange("(g p t) -> p g t", p=P, t=PACK))
+        nc.vector.memset(gain_row[:], 0.0)
+        nc.scalar.dma_start(out=gain_row[0:1, :], in_=norm_query_w.rearrange("(o k) -> o k", o=1))
+        nc.vector.memset(ones[:], 1.0)
         nc.vector.memset(eps[:], EPS)
         nc.scalar.activation(out=table_warm[:], in_=eps[:], func=ACT.Sqrt)
         make_identity(nc, identity[:])
@@ -154,21 +176,22 @@ def tile_hopfieldmemorylayer_pa_kernel(tc, query_input, norm_query_w, W_in_words
         for i in range(3, ROW_TILES):
             load_rows(i)
 
+        spread_gain()
         rms = {0: statistics(0), 1: statistics(1)}
-        y = {0: normalise(0, rms[0])}
-        banks = transpose(y[0])
-        h = gain(banks)
-        y[1] = normalise(1, rms[1])
+        h_sorted = {0: normalise(0, rms[0])}
+        banks = transpose(h_sorted[0])
+        h = gather(banks)
+        h_sorted[1] = normalise(1, rms[1])
         quantised = {0: quantise(h)}
         for i in range(ROW_TILES):
             if i + 1 < ROW_TILES:
-                banks = transpose(y[i + 1])
+                banks = transpose(h_sorted[i + 1])
             if i + 2 < ROW_TILES:
                 rms[i + 2] = statistics(i + 2)
             if i + 1 < ROW_TILES:
-                h = gain(banks)
+                h = gather(banks)
             if i + 2 < ROW_TILES:
-                y[i + 2] = normalise(i + 2, rms[i + 2])
+                h_sorted[i + 2] = normalise(i + 2, rms[i + 2])
             if i + 1 < ROW_TILES:
                 quantised[i + 1] = quantise(h)
             project(i, quantised[i][0], quantised[i][1])

@@ -25,7 +25,9 @@ N_TILE = 512
 N_TILES = FEATURES // N_TILE
 SCALE_ROWS = 4
 QUADRANTS = 4
-PASSES_A_BANK = 2
+DUO = 2
+DUOS = PASSES // DUO
+QUARTERS = 4
 EPS = 1e-6
 
 FLOPS = 2 * ROWS * FEATURES * FEATURES
@@ -38,28 +40,41 @@ def tile_hopfieldmemorylayer_pa_kernel(tc, query_input, norm_query_w, W_in_words
 
     with ExitStack() as ctx:
         keep = ctx.enter_context(tc.tile_pool(name="keep", bufs=1))
-        stats_pool = ctx.enter_context(tc.tile_pool(name="stats", bufs=4))
         work = ctx.enter_context(tc.tile_pool(name="work", bufs=2))
-        results = ctx.enter_context(tc.tile_pool(name="results", bufs=3))
-        turned = ctx.enter_context(tc.psum_pool(name="turned", bufs=4))
+        gain_psum = ctx.enter_context(tc.psum_pool(name="gain_psum", bufs=1))
+        turned = ctx.enter_context(tc.psum_pool(name="turned", bufs=DUOS))
         sums = ctx.enter_context(tc.psum_pool(name="sums", bufs=N_TILES))
         ctx.enter_context(tc.manual_schedule())
 
         x_all = keep.tile([P, ROW_TILES, FEATURES], BF16)
         w_codes = keep.tile([P, PASSES, FEATURES], U32, align_bytes=64)
         w_planes = keep.tile([P, FEATURES], U8, align_bytes=64)
-        gain_row = keep.tile([P, FEATURES], BF16)
-        gain_sorted = keep.tile([P, HALVES, PASSES, P, PAIR], BF16)
-        ones = keep.tile([P, P], BF16)
+        h_codes = keep.tile([P, ROW_TILES, PASSES, P], U32, align_bytes=64)
+        h_planes = keep.tile([P, ROW_TILES, PASSES, P], U8, align_bytes=64)
+        result = keep.tile([P, ROW_TILES, FEATURES], F32)
+        gain_words = keep.tile([P, PASSES, PACK], BF16)
         identity = keep.tile([P, P], F32)
+        identity_bf = keep.tile([P, P], BF16)
         eps = keep.tile([P, 1], F32)
         table_warm = keep.tile([P, 1], F32)
+        squares_s = keep.tile([P, FEATURES], BF16)
+        squares_v = keep.tile([P, FEATURES // QUARTERS], BF16)
+        first_sums = keep.tile([P, QUARTERS], F32)
+        sum_squares = keep.tile([P, ROW_TILES], F32)
+        first_sum = keep.tile([P, 1], F32)
+        rms = keep.tile([P, ROW_TILES], F32)
+        inv_rms = keep.tile([P, ROW_TILES], F32)
+        gain_banks = [gain_psum.tile([P, HALVES, PAIR, DUO * P], BF16, name="gain_bank%d" % b) for b in range(DUOS)]
 
         def load_rows(i):
             nc.sync.dma_start(out=x_all[:, i, :], in_=x_rows[i * P : (i + 1) * P, :])
 
+        def load_first_rows():
+            width = FEATURES // QUARTERS
+            for q in range(QUARTERS):
+                nc.sync.dma_start(out=x_all[:, 0, q * width : (q + 1) * width], in_=x_rows[0:P, q * width : (q + 1) * width])
+
         def load_weight_scales():
-            nc.vector.memset(w_planes[:].bitcast(I32), 0)
             for quadrant in range(QUADRANTS):
                 first = 32 * quadrant
                 nc.sync.dma_start(
@@ -76,122 +91,200 @@ def tile_hopfieldmemorylayer_pa_kernel(tc, query_input, norm_query_w, W_in_words
 
         def spread_gain():
             for g in range(PASSES):
-                acc = sums.tile([P, N_TILE], F32, name="acc")
-                nc.tensor.matmul(out=acc[:], lhsT=ones[:], rhs=gain_row[:, g * K_PASS : (g + 1) * K_PASS], start=True, stop=True)
-                nc.vector.tensor_copy(
-                    out=gain_sorted[:, :, g, :, :],
-                    in_=acc[:].rearrange("r (p u e) -> r u p e", u=HALVES, e=PAIR),
-                )
+                for t in range(PACK):
+                    first = (g % DUO) * P
+                    nc.tensor.matmul(
+                        out=gain_banks[g // DUO][:, t // PAIR, t % PAIR, first : first + P],
+                        lhsT=gain_words[:, g, t : t + 1].to_broadcast([P, P]),
+                        rhs=identity_bf[:],
+                        start=True,
+                        stop=True,
+                    )
+
+        def first_statistics():
+            width = FEATURES // QUARTERS
+            for q in range(QUARTERS):
+                piece = x_all[:, 0, q * width : (q + 1) * width]
+                if q % 2 == 0:
+                    nc.scalar.activation(out=squares_s[:, 0:width], in_=piece, func=ACT.Square, accum_out=first_sums[:, q : q + 1])
+                else:
+                    nc.vector.scalar_tensor_tensor(
+                        out=squares_v[:], in0=piece, scalar=1.0, in1=piece, op0=ALU.mult, op1=ALU.mult,
+                        accum_out=first_sums[:, q : q + 1],
+                    )
+            nc.vector.tensor_reduce(out=first_sum[:], in_=first_sums[:], axis=mybir.AxisListType.X, op=ALU.add)
+            nc.scalar.activation(out=rms[:, 0:1], in_=first_sum[:], func=ACT.Sqrt, scale=1.0 / FEATURES, bias=eps[:])
 
         def statistics(i):
-            squares = work.tile([P, FEATURES], BF16)
-            sum_squares = stats_pool.tile([P, 1], F32)
-            nc.scalar.activation(out=squares[:], in_=x_all[:, i, :], func=ACT.Square, accum_out=sum_squares[:])
-            rms = stats_pool.tile([P, 1], F32)
-            nc.scalar.activation(out=rms[:], in_=sum_squares[:], func=ACT.Sqrt, scale=1.0 / FEATURES, bias=eps[:])
-            return rms
+            nc.scalar.activation(out=squares_s[:], in_=x_all[:, i, :], func=ACT.Square, accum_out=sum_squares[:, i : i + 1])
+            nc.scalar.activation(out=rms[:, i : i + 1], in_=sum_squares[:, i : i + 1], func=ACT.Sqrt, scale=1.0 / FEATURES, bias=eps[:])
 
-        def normalise(i, rms):
-            inv_rms = stats_pool.tile([P, 1], F32)
-            nc.vector.reciprocal(inv_rms[:], rms[:])
-            h_sorted = work.tile([P, HALVES, PASSES * P, PAIR], BF16)
-            pairs = x_all[:, i, :].rearrange("r (c u e) -> r u c e", u=HALVES, e=PAIR)
-            for u in range(HALVES):
+        def invert(i):
+            nc.vector.reciprocal(inv_rms[:, i : i + 1], rms[:, i : i + 1])
+
+        h_sorted = {}
+
+        def normalise(i, b, halves=(0, 1)):
+            if i not in h_sorted:
+                h_sorted[i] = work.tile([P, DUOS, HALVES, DUO * P, PAIR], BF16, name="h_sorted")
+            pairs = x_all[:, i, b * DUO * K_PASS : (b + 1) * DUO * K_PASS].rearrange("r (c u e) -> r u c e", u=HALVES, e=PAIR)
+            for u in halves:
                 nc.vector.scalar_tensor_tensor(
-                    out=h_sorted[:, u, :, :],
+                    out=h_sorted[i][:, b, u, :, :],
                     in0=pairs[:, u, :, :],
-                    scalar=inv_rms[:],
-                    in1=gain_sorted[:, u, :, :, :].rearrange("r g p e -> r (g p) e"),
+                    scalar=inv_rms[:, i : i + 1],
+                    in1=gain_banks[b][:, u, :, :].rearrange("r e c -> r c e"),
                     op0=ALU.mult,
                     op1=ALU.mult,
                 )
-            return h_sorted
 
-        def transpose(h_sorted):
-            words = h_sorted[:].rearrange("r u c e -> r (u c e)").bitcast(F32)
-            banks = []
-            for b in range(PASSES // PASSES_A_BANK):
-                bank = turned.tile([P, PASSES_A_BANK, HALVES, P], F32, name="bank")
-                for j in range(PASSES_A_BANK):
-                    g = b * PASSES_A_BANK + j
-                    for u in range(HALVES):
-                        first = (u * PASSES + g) * P
-                        nc.tensor.transpose(bank[:, j, u, :], words[:, first : first + P], identity[:])
-                banks.append(bank)
-            return banks
+        banks = {}
 
-        def gather(banks):
-            h = work.tile([P, PASSES, P, PACK], BF16, align_bytes=64)
-            h_words = h[:].rearrange("p g r t -> p (g r t)").bitcast(F32).rearrange("p (g r u) -> p g r u", g=PASSES, u=HALVES)
-            for b in range(PASSES // PASSES_A_BANK):
-                nc.vector.tensor_copy(
-                    out=h_words[:, b * PASSES_A_BANK : (b + 1) * PASSES_A_BANK, :, :],
-                    in_=banks[b][:].rearrange("p g u r -> p g r u"),
-                )
-            return h
+        def transpose(i, b):
+            words = h_sorted[i][:].rearrange("r b u c e -> r (b u c e)").bitcast(F32)
+            bank = turned.tile([P, DUO, HALVES, P], F32, name="bank")
+            for j in range(DUO):
+                for u in range(HALVES):
+                    first = ((b * HALVES + u) * DUO + j) * P
+                    nc.tensor.transpose(bank[:, j, u, :], words[:, first : first + P], identity[:])
+            banks[(i, b)] = bank
 
-        def quantise(h):
-            h_codes = work.tile([P, PASSES, P], U32, align_bytes=64)
-            h_planes = work.tile([P, PASSES, P], U8, align_bytes=64)
+        h = {}
+
+        def gather(i, b, engine):
+            if i not in h:
+                h[i] = work.tile([P, PASSES, P, PACK], BF16, align_bytes=64, name="h")
+            h_words = h[i][:].rearrange("p g r t -> p (g r t)").bitcast(F32).rearrange("p (g r u) -> p g r u", g=PASSES, u=HALVES)
+            dst = h_words[:, b * DUO : (b + 1) * DUO, :, :]
+            src = banks[(i, b)][:].rearrange("p g u r -> p g r u")
+            if engine == "scalar":
+                nc.scalar.copy(out=dst, in_=src)
+            else:
+                nc.vector.tensor_copy(out=dst, in_=src)
+
+        def quantise(i, first_pass, passes):
+            chosen = slice(first_pass, first_pass + passes)
             nc.vector.quantize_mx(
-                out=h_codes[:].rearrange("p g r -> p (g r)").bitcast(FP8X4),
-                scales=h_planes[:].rearrange("p g r -> p (g r)"),
-                in_=h[:].rearrange("p g r t -> p (g r t)"),
+                out=h_codes[:, i, chosen, :].rearrange("p g r -> p (g r)").bitcast(FP8X4),
+                scales=h_planes[:, i, chosen, :].rearrange("p g r -> p (g r)"),
+                in_=h[i][:, chosen, :, :].rearrange("p g r t -> p (g r t)"),
             )
-            return h_codes, h_planes
 
-        def project(i, h_codes, h_planes):
-            result = results.tile([P, FEATURES], F32)
-            for n in range(N_TILES):
-                n_cols = slice(n * N_TILE, (n + 1) * N_TILE)
-                acc = sums.tile([P, N_TILE], F32, name="acc")
-                for g in range(PASSES):
-                    nc.tensor.matmul_mx(
-                        out=acc[:],
-                        lhsT=h_codes[:, g, :].bitcast(FP8X4),
-                        lhsT_scale=h_planes[:, g, :],
-                        rhs=w_codes[:, g, n_cols].bitcast(FP8X4),
-                        rhs_scale=w_planes[SCALE_ROWS * g : P, n_cols],
-                        start=(g == 0),
-                        stop=(g == PASSES - 1),
-                    )
-                nc.scalar.copy(out=result[:, n_cols], in_=acc[:])
-                nc.sync.dma_start(out=out_rows[i * P : (i + 1) * P, n_cols], in_=result[:, n_cols])
+        open_banks = {}
 
-        nc.vector.memset(gain_row[:], 0.0)
-        nc.scalar.dma_start(out=gain_row[0:1, :], in_=norm_query_w.rearrange("(o k) -> o k", o=1))
-        nc.vector.memset(ones[:], 1.0)
+        def project(i, n):
+            n_cols = slice(n * N_TILE, (n + 1) * N_TILE)
+            acc = sums.tile([P, N_TILE], F32, name="acc")
+            for g in range(PASSES):
+                nc.tensor.matmul_mx(
+                    out=acc[:],
+                    lhsT=h_codes[:, i, g, :].bitcast(FP8X4),
+                    lhsT_scale=h_planes[:, i, g, :],
+                    rhs=w_codes[:, g, n_cols].bitcast(FP8X4),
+                    rhs_scale=w_planes[SCALE_ROWS * g : P, n_cols],
+                    start=(g == 0),
+                    stop=(g == PASSES - 1),
+                )
+            open_banks[(i, n)] = acc
+
+        def empty(i, n, engine):
+            n_cols = slice(n * N_TILE, (n + 1) * N_TILE)
+            if engine == "scalar":
+                nc.scalar.copy(out=result[:, i, n_cols], in_=open_banks[(i, n)][:])
+            else:
+                nc.vector.tensor_copy(out=result[:, i, n_cols], in_=open_banks[(i, n)][:])
+            nc.sync.dma_start(out=out_rows[i * P : (i + 1) * P, n_cols], in_=result[:, i, n_cols])
+
+        with nc.allow_non_contiguous_dma(reason="the gain, four neighbouring features to a partition"):
+            nc.scalar.dma_start(out=gain_words[:], in_=norm_query_w.rearrange("(g p t) -> p g t", p=P, t=PACK))
+        nc.vector.memset(w_planes[:].bitcast(I32), 0)
         nc.vector.memset(eps[:], EPS)
         nc.scalar.activation(out=table_warm[:], in_=eps[:], func=ACT.Sqrt)
+        make_identity(nc, identity_bf[:])
         make_identity(nc, identity[:])
-
-        load_rows(0)
+        load_first_rows()
         load_rows(1)
-        load_weight_scales()
-        load_weight_columns(0)
-        load_weight_columns(1)
         load_rows(2)
-        load_weight_columns(2)
-        load_weight_columns(3)
+        load_weight_scales()
+        for n in range(N_TILES):
+            load_weight_columns(n)
         for i in range(3, ROW_TILES):
             load_rows(i)
 
         spread_gain()
-        rms = {0: statistics(0), 1: statistics(1)}
-        h_sorted = {0: normalise(0, rms[0])}
-        banks = transpose(h_sorted[0])
-        h = gather(banks)
-        h_sorted[1] = normalise(1, rms[1])
-        quantised = {0: quantise(h)}
-        for i in range(ROW_TILES):
+        first_statistics()
+        invert(0)
+        statistics(1)
+        normalise(0, 0)
+        transpose(0, 0)
+        gather(0, 0, "scalar")
+        normalise(0, 1)
+        transpose(0, 1)
+        gather(0, 1, "scalar")
+        invert(1)
+        normalise(1, 0, (0,))
+        quantise(0, 0, DUO)
+        normalise(1, 0, (1,))
+        quantise(0, DUO, DUO)
+        normalise(1, 1)
+        statistics(2)
+
+        project(0, 0)
+        transpose(1, 0)
+        project(0, 1)
+        transpose(1, 1)
+        project(0, 2)
+        gather(1, 0, "scalar")
+        empty(0, 0, "scalar")
+        gather(1, 1, "scalar")
+        empty(0, 1, "scalar")
+        invert(2)
+        normalise(2, 0)
+        quantise(1, 0, DUO)
+        quantise(1, DUO, DUO)
+        normalise(2, 1)
+        empty(0, 2, "scalar")
+        statistics(3)
+
+        project(1, 0)
+        transpose(2, 0)
+        transpose(2, 1)
+        project(1, 1)
+        project(1, 2)
+        project(0, 3)
+        empty(1, 0, "scalar")
+        project(1, 3)
+        gather(2, 0, "vector")
+        gather(2, 1, "vector")
+        invert(3)
+        normalise(3, 0)
+        normalise(3, 1)
+        quantise(2, 0, PASSES)
+        empty(1, 1, "scalar")
+        empty(1, 2, "scalar")
+        statistics(4)
+        empty(0, 3, "scalar")
+        left = (1, 3)
+
+        for i in range(2, ROW_TILES):
             if i + 1 < ROW_TILES:
-                banks = transpose(h_sorted[i + 1])
+                transpose(i + 1, 0)
+                transpose(i + 1, 1)
+            empty(left[0], left[1], "vector")
+            left = (i, N_TILES - 1)
+            for n in range(N_TILES):
+                project(i, n)
+            if i + 1 < ROW_TILES:
+                gather(i + 1, 0, "vector")
+                gather(i + 1, 1, "vector")
             if i + 2 < ROW_TILES:
-                rms[i + 2] = statistics(i + 2)
+                invert(i + 2)
+                normalise(i + 2, 0)
+                normalise(i + 2, 1)
             if i + 1 < ROW_TILES:
-                h = gather(banks)
-            if i + 2 < ROW_TILES:
-                h_sorted[i + 2] = normalise(i + 2, rms[i + 2])
-            if i + 1 < ROW_TILES:
-                quantised[i + 1] = quantise(h)
-            project(i, quantised[i][0], quantised[i][1])
+                quantise(i + 1, 0, PASSES)
+            if i + 3 < ROW_TILES:
+                statistics(i + 3)
+            for n in range(N_TILES - 1):
+                empty(i, n, "scalar")
+        empty(left[0], left[1], "vector")

@@ -54,17 +54,17 @@ def tile_hopfieldmemorylayer_pa_kernel(tc, query_input, norm_query_w, W_in_words
         result = keep.tile([P, ROW_TILES, FEATURES], F32)
         gain_words = keep.tile([P, PASSES, PACK], BF16)
         identity = keep.tile([P, P], F32)
-        identity_bf = keep.tile([P, P], BF16)
         eps = keep.tile([P, 1], F32)
         table_warm = keep.tile([P, 1], F32)
         squares_s = keep.tile([P, FEATURES], BF16)
         squares_v = keep.tile([P, FEATURES // QUARTERS], BF16)
         first_sums = keep.tile([P, QUARTERS], F32)
+        first_copy = keep.tile([P, QUARTERS], F32)
         sum_squares = keep.tile([P, ROW_TILES], F32)
         first_sum = keep.tile([P, 1], F32)
         rms = keep.tile([P, ROW_TILES], F32)
         inv_rms = keep.tile([P, ROW_TILES], F32)
-        gain_banks = [gain_psum.tile([P, HALVES, PAIR, DUO * P], BF16, name="gain_bank%d" % b) for b in range(DUOS)]
+        gain_banks = [gain_psum.tile([P, HALVES, DUO * P], F32, name="gain_bank%d" % b) for b in range(DUOS)]
 
         def load_rows(i):
             nc.sync.dma_start(out=x_all[:, i, :], in_=x_rows[i * P : (i + 1) * P, :])
@@ -90,29 +90,28 @@ def tile_hopfieldmemorylayer_pa_kernel(tc, query_input, norm_query_w, W_in_words
             )
 
         def spread_gain():
+            words = gain_words[:].rearrange("p g t -> p (g t)").bitcast(F32)
             for g in range(PASSES):
-                for t in range(PACK):
+                for u in range(HALVES):
                     first = (g % DUO) * P
-                    nc.tensor.matmul(
-                        out=gain_banks[g // DUO][:, t // PAIR, t % PAIR, first : first + P],
-                        lhsT=gain_words[:, g, t : t + 1].to_broadcast([P, P]),
-                        rhs=identity_bf[:],
-                        start=True,
-                        stop=True,
+                    nc.tensor.transpose(
+                        gain_banks[g // DUO][:, u, first : first + P],
+                        words[:, g * HALVES + u : g * HALVES + u + 1].to_broadcast([P, P]),
+                        identity[:],
                     )
 
         def first_statistics():
             width = FEATURES // QUARTERS
             for q in range(QUARTERS):
                 piece = x_all[:, 0, q * width : (q + 1) * width]
-                if q % 2 == 0:
+                if q >= QUARTERS // 2:
                     nc.scalar.activation(out=squares_s[:, 0:width], in_=piece, func=ACT.Square, accum_out=first_sums[:, q : q + 1])
                 else:
                     nc.vector.scalar_tensor_tensor(
                         out=squares_v[:], in0=piece, scalar=1.0, in1=piece, op0=ALU.mult, op1=ALU.mult,
                         accum_out=first_sums[:, q : q + 1],
                     )
-            nc.vector.tensor_reduce(out=first_sum[:], in_=first_sums[:], axis=mybir.AxisListType.X, op=ALU.add)
+            nc.scalar.activation(out=first_copy[:], in_=first_sums[:], func=ACT.Copy, accum_out=first_sum[:])
             nc.scalar.activation(out=rms[:, 0:1], in_=first_sum[:], func=ACT.Sqrt, scale=1.0 / FEATURES, bias=eps[:])
 
         def statistics(i):
@@ -133,7 +132,7 @@ def tile_hopfieldmemorylayer_pa_kernel(tc, query_input, norm_query_w, W_in_words
                     out=h_sorted[i][:, b, u, :, :],
                     in0=pairs[:, u, :, :],
                     scalar=inv_rms[:, i : i + 1],
-                    in1=gain_banks[b][:, u, :, :].rearrange("r e c -> r c e"),
+                    in1=gain_banks[b][:, u, :].bitcast(BF16).rearrange("r (c e) -> r c e", e=PAIR),
                     op0=ALU.mult,
                     op1=ALU.mult,
                 )
@@ -143,8 +142,8 @@ def tile_hopfieldmemorylayer_pa_kernel(tc, query_input, norm_query_w, W_in_words
         def transpose(i, b):
             words = h_sorted[i][:].rearrange("r b u c e -> r (b u c e)").bitcast(F32)
             bank = turned.tile([P, DUO, HALVES, P], F32, name="bank")
-            for j in range(DUO):
-                for u in range(HALVES):
+            for u in range(HALVES):
+                for j in range(DUO):
                     first = ((b * HALVES + u) * DUO + j) * P
                     nc.tensor.transpose(bank[:, j, u, :], words[:, first : first + P], identity[:])
             banks[(i, b)] = bank
@@ -172,10 +171,12 @@ def tile_hopfieldmemorylayer_pa_kernel(tc, query_input, norm_query_w, W_in_words
 
         open_banks = {}
 
-        def project(i, n):
-            n_cols = slice(n * N_TILE, (n + 1) * N_TILE)
-            acc = sums.tile([P, N_TILE], F32, name="acc")
-            for g in range(PASSES):
+        def project(i, n, first=0, width=N_TILE, passes=(0, 1, 2, 3)):
+            n_cols = slice(n * N_TILE + first, n * N_TILE + first + width)
+            if passes[0] == 0:
+                open_banks[(i, n, first)] = sums.tile([P, width], F32, name="acc")
+            acc = open_banks[(i, n, first)]
+            for g in passes:
                 nc.tensor.matmul_mx(
                     out=acc[:],
                     lhsT=h_codes[:, i, g, :].bitcast(FP8X4),
@@ -185,14 +186,13 @@ def tile_hopfieldmemorylayer_pa_kernel(tc, query_input, norm_query_w, W_in_words
                     start=(g == 0),
                     stop=(g == PASSES - 1),
                 )
-            open_banks[(i, n)] = acc
 
-        def empty(i, n, engine):
-            n_cols = slice(n * N_TILE, (n + 1) * N_TILE)
+        def empty(i, n, engine, first=0, width=N_TILE):
+            n_cols = slice(n * N_TILE + first, n * N_TILE + first + width)
             if engine == "scalar":
-                nc.scalar.copy(out=result[:, i, n_cols], in_=open_banks[(i, n)][:])
+                nc.scalar.copy(out=result[:, i, n_cols], in_=open_banks[(i, n, first)][:])
             else:
-                nc.vector.tensor_copy(out=result[:, i, n_cols], in_=open_banks[(i, n)][:])
+                nc.vector.tensor_copy(out=result[:, i, n_cols], in_=open_banks[(i, n, first)][:])
             nc.sync.dma_start(out=out_rows[i * P : (i + 1) * P, n_cols], in_=result[:, i, n_cols])
 
         with nc.allow_non_contiguous_dma(reason="the gain, four neighbouring features to a partition"):
@@ -200,15 +200,16 @@ def tile_hopfieldmemorylayer_pa_kernel(tc, query_input, norm_query_w, W_in_words
         nc.vector.memset(w_planes[:].bitcast(I32), 0)
         nc.vector.memset(eps[:], EPS)
         nc.scalar.activation(out=table_warm[:], in_=eps[:], func=ACT.Sqrt)
-        make_identity(nc, identity_bf[:])
         make_identity(nc, identity[:])
         load_first_rows()
         load_rows(1)
         load_rows(2)
         load_weight_scales()
-        for n in range(N_TILES):
+        for n in range(N_TILES - 1):
             load_weight_columns(n)
-        for i in range(3, ROW_TILES):
+        load_rows(3)
+        load_weight_columns(N_TILES - 1)
+        for i in range(4, ROW_TILES):
             load_rows(i)
 
         spread_gain()
@@ -229,8 +230,9 @@ def tile_hopfieldmemorylayer_pa_kernel(tc, query_input, norm_query_w, W_in_words
         normalise(1, 1)
         statistics(2)
 
-        project(0, 0)
+        project(0, 0, passes=(0, 1))
         transpose(1, 0)
+        project(0, 0, passes=(2, 3))
         project(0, 1)
         transpose(1, 1)
         project(0, 2)
@@ -266,7 +268,7 @@ def tile_hopfieldmemorylayer_pa_kernel(tc, query_input, norm_query_w, W_in_words
         empty(0, 3, "scalar")
         left = (1, 3)
 
-        for i in range(2, ROW_TILES):
+        for i in range(2, ROW_TILES - 1):
             if i + 1 < ROW_TILES:
                 transpose(i + 1, 0)
                 transpose(i + 1, 1)
@@ -287,4 +289,16 @@ def tile_hopfieldmemorylayer_pa_kernel(tc, query_input, norm_query_w, W_in_words
                 statistics(i + 3)
             for n in range(N_TILES - 1):
                 empty(i, n, "scalar")
+
+        i = ROW_TILES - 1
+        half = N_TILE // 2
         empty(left[0], left[1], "vector")
+        for n in range(N_TILES - 1):
+            project(i, n)
+        project(i, N_TILES - 1, 0, half)
+        empty(i, 0, "scalar")
+        project(i, N_TILES - 1, half, half)
+        empty(i, 1, "vector")
+        empty(i, 2, "scalar")
+        empty(i, N_TILES - 1, "vector", 0, half)
+        empty(i, N_TILES - 1, "scalar", half, half)

@@ -56,6 +56,7 @@ def tile_hopfieldmemorylayer_pa_kernel(tc, query_input, norm_query_w, W_in_words
         identity = keep.tile([P, P], F32)
         eps = keep.tile([P, 1], F32)
         table_warm = keep.tile([P, 1], F32)
+        idle_rhs = keep.tile([P, N_TILE], BF16)
         squares_s = keep.tile([P, FEATURES], BF16)
         squares_v = keep.tile([P, FEATURES // QUARTERS], BF16)
         first_sums = keep.tile([P, QUARTERS], F32)
@@ -99,6 +100,10 @@ def tile_hopfieldmemorylayer_pa_kernel(tc, query_input, norm_query_w, W_in_words
                         words[:, g * HALVES + u : g * HALVES + u + 1].to_broadcast([P, P]),
                         identity[:],
                     )
+
+        def keep_clock_up(count):
+            for j in range(count):
+                nc.tensor.matmul(out=idle_bank[:], lhsT=idle_rhs[:, 0:P], rhs=idle_rhs[:], start=True, stop=True)
 
         def first_statistics():
             width = FEATURES // QUARTERS
@@ -200,6 +205,7 @@ def tile_hopfieldmemorylayer_pa_kernel(tc, query_input, norm_query_w, W_in_words
         nc.vector.memset(w_planes[:].bitcast(I32), 0)
         nc.vector.memset(eps[:], EPS)
         nc.scalar.activation(out=table_warm[:], in_=eps[:], func=ACT.Sqrt)
+        nc.gpsimd.memset(idle_rhs[:], 0.0)
         make_identity(nc, identity[:])
         load_first_rows()
         load_rows(1)
@@ -213,14 +219,18 @@ def tile_hopfieldmemorylayer_pa_kernel(tc, query_input, norm_query_w, W_in_words
             load_rows(i)
 
         spread_gain()
+        idle_bank = sums.tile([P, N_TILE], F32, name="acc")
+        keep_clock_up(3)
         first_statistics()
         invert(0)
         statistics(1)
         normalise(0, 0)
         transpose(0, 0)
+        keep_clock_up(2)
         gather(0, 0, "scalar")
         normalise(0, 1)
         transpose(0, 1)
+        keep_clock_up(2)
         gather(0, 1, "scalar")
         invert(1)
         normalise(1, 0, (0,))
@@ -233,8 +243,9 @@ def tile_hopfieldmemorylayer_pa_kernel(tc, query_input, norm_query_w, W_in_words
         project(0, 0, passes=(0, 1))
         transpose(1, 0)
         project(0, 0, passes=(2, 3))
-        project(0, 1)
+        project(0, 1, passes=(0, 1))
         transpose(1, 1)
+        project(0, 1, passes=(2, 3))
         project(0, 2)
         gather(1, 0, "scalar")
         empty(0, 0, "scalar")

@@ -52,8 +52,9 @@ def tile_hopfieldmemorylayer_pa_kernel(tc, query_input, norm_query_w, W_in_words
         h_codes = keep.tile([P, ROW_TILES, PASSES, P], U32, align_bytes=64)
         h_planes = keep.tile([P, ROW_TILES, PASSES, P], U8, align_bytes=64)
         result = keep.tile([P, ROW_TILES, FEATURES], F32)
-        gain_words = keep.tile([P, PASSES, PACK], BF16)
+        gain_rows = keep.tile([P, K_PASS], BF16)
         identity = keep.tile([P, P], F32)
+        identity_bf = keep.tile([P, P], BF16)
         eps = keep.tile([P, 1], F32)
         table_warm = keep.tile([P, 1], F32)
         idle_rhs = keep.tile([P, N_TILE], BF16)
@@ -65,7 +66,7 @@ def tile_hopfieldmemorylayer_pa_kernel(tc, query_input, norm_query_w, W_in_words
         first_sum = keep.tile([P, 1], F32)
         rms = keep.tile([P, ROW_TILES], F32)
         inv_rms = keep.tile([P, ROW_TILES], F32)
-        gain_banks = [gain_psum.tile([P, HALVES, DUO * P], F32, name="gain_bank%d" % b) for b in range(DUOS)]
+        gain_banks = [gain_psum.tile([P, DUO * K_PASS], BF16, name="gain_bank%d" % b) for b in range(DUOS)]
 
         def load_rows(i):
             nc.sync.dma_start(out=x_all[:, i, :], in_=x_rows[i * P : (i + 1) * P, :])
@@ -91,15 +92,15 @@ def tile_hopfieldmemorylayer_pa_kernel(tc, query_input, norm_query_w, W_in_words
             )
 
         def spread_gain():
-            words = gain_words[:].rearrange("p g t -> p (g t)").bitcast(F32)
             for g in range(PASSES):
-                for u in range(HALVES):
-                    first = (g % DUO) * P
-                    nc.tensor.transpose(
-                        gain_banks[g // DUO][:, u, first : first + P],
-                        words[:, g * HALVES + u : g * HALVES + u + 1].to_broadcast([P, P]),
-                        identity[:],
-                    )
+                first = (g % DUO) * K_PASS
+                nc.tensor.matmul(
+                    out=gain_banks[g // DUO][:, first : first + K_PASS],
+                    lhsT=identity_bf[:, g : g + 1].to_broadcast([P, P]),
+                    rhs=gain_rows[:],
+                    start=True,
+                    stop=True,
+                )
 
         def keep_clock_up(count):
             for j in range(count):
@@ -137,7 +138,7 @@ def tile_hopfieldmemorylayer_pa_kernel(tc, query_input, norm_query_w, W_in_words
                     out=h_sorted[i][:, b, u, :, :],
                     in0=pairs[:, u, :, :],
                     scalar=inv_rms[:, i : i + 1],
-                    in1=gain_banks[b][:, u, :].bitcast(BF16).rearrange("r (c e) -> r c e", e=PAIR),
+                    in1=gain_banks[b][:].rearrange("r (c u e) -> r u c e", u=HALVES, e=PAIR)[:, u, :, :],
                     op0=ALU.mult,
                     op1=ALU.mult,
                 )
@@ -200,14 +201,15 @@ def tile_hopfieldmemorylayer_pa_kernel(tc, query_input, norm_query_w, W_in_words
                 nc.vector.tensor_copy(out=result[:, i, n_cols], in_=open_banks[(i, n, first)][:])
             nc.sync.dma_start(out=out_rows[i * P : (i + 1) * P, n_cols], in_=result[:, i, n_cols])
 
-        with nc.allow_non_contiguous_dma(reason="the gain, four neighbouring features to a partition"):
-            nc.scalar.dma_start(out=gain_words[:], in_=norm_query_w.rearrange("(g p t) -> p g t", p=P, t=PACK))
+        nc.gpsimd.memset(gain_rows[:], 0.0)
         nc.vector.memset(w_planes[:].bitcast(I32), 0)
         nc.vector.memset(eps[:], EPS)
         nc.scalar.activation(out=table_warm[:], in_=eps[:], func=ACT.Sqrt)
+        make_identity(nc, identity_bf[:])
         nc.gpsimd.memset(idle_rhs[:], 0.0)
         make_identity(nc, identity[:])
         load_first_rows()
+        nc.sync.dma_start(out=gain_rows[0:PASSES, :], in_=norm_query_w.rearrange("(g j) -> g j", g=PASSES))
         load_rows(1)
         load_rows(2)
         load_weight_scales()

@@ -57,7 +57,6 @@ def tile_hopfieldmemorylayer_pa_kernel(tc, query_input, norm_query_w, W_in_words
         identity_bf = keep.tile([P, P], BF16)
         eps = keep.tile([P, 1], F32)
         table_warm = keep.tile([P, 1], F32)
-        idle_rhs = keep.tile([P, N_TILE], BF16)
         squares_s = keep.tile([P, FEATURES], BF16)
         squares_v = keep.tile([P, FEATURES // QUARTERS], BF16)
         first_sums = keep.tile([P, QUARTERS], F32)
@@ -101,10 +100,6 @@ def tile_hopfieldmemorylayer_pa_kernel(tc, query_input, norm_query_w, W_in_words
                     start=True,
                     stop=True,
                 )
-
-        def keep_clock_up(count):
-            for j in range(count):
-                nc.tensor.matmul(out=idle_bank[:], lhsT=idle_rhs[:, 0:P], rhs=idle_rhs[:], start=True, stop=True)
 
         def first_statistics():
             width = FEATURES // QUARTERS
@@ -206,7 +201,6 @@ def tile_hopfieldmemorylayer_pa_kernel(tc, query_input, norm_query_w, W_in_words
         nc.vector.memset(eps[:], EPS)
         nc.scalar.activation(out=table_warm[:], in_=eps[:], func=ACT.Sqrt)
         make_identity(nc, identity_bf[:])
-        nc.gpsimd.memset(idle_rhs[:], 0.0)
         make_identity(nc, identity[:])
         load_first_rows()
         nc.sync.dma_start(out=gain_rows[0:PASSES, :], in_=norm_query_w.rearrange("(g j) -> g j", g=PASSES))
@@ -221,18 +215,14 @@ def tile_hopfieldmemorylayer_pa_kernel(tc, query_input, norm_query_w, W_in_words
             load_rows(i)
 
         spread_gain()
-        idle_bank = sums.tile([P, N_TILE], F32, name="acc")
-        keep_clock_up(3)
         first_statistics()
         invert(0)
         statistics(1)
         normalise(0, 0)
         transpose(0, 0)
-        keep_clock_up(2)
         gather(0, 0, "scalar")
         normalise(0, 1)
         transpose(0, 1)
-        keep_clock_up(2)
         gather(0, 1, "scalar")
         invert(1)
         normalise(1, 0, (0,))

@@ -83,11 +83,12 @@ def tile_hopfieldmemorylayer_pa_kernel(tc, query_input, norm_query_w, W_in_words
                     in_=W_in_scales[:, SCALE_ROWS * quadrant : SCALE_ROWS * (quadrant + 1), :].bitcast(I32),
                 )
 
-        def load_weight_columns(n):
+        def load_weight_columns(n, first=0, width=N_TILE):
             words = W_in_words.rearrange("g p n t -> p g (n t)")
+            start = n * N_TILE + first
             nc.sync.dma_start(
-                out=w_codes[:, :, n * N_TILE : (n + 1) * N_TILE].bitcast(I32),
-                in_=words[:, :, n * N_TILE * PACK : (n + 1) * N_TILE * PACK].bitcast(I32),
+                out=w_codes[:, :, start : start + width].bitcast(I32),
+                in_=words[:, :, start * PACK : (start + width) * PACK].bitcast(I32),
             )
 
         def spread_gain():
@@ -207,8 +208,10 @@ def tile_hopfieldmemorylayer_pa_kernel(tc, query_input, norm_query_w, W_in_words
         load_rows(1)
         load_rows(2)
         load_weight_scales()
-        for n in range(N_TILES - 1):
-            load_weight_columns(n)
+        load_weight_columns(0)
+        load_weight_columns(1)
+        load_weight_columns(2, 0, N_TILE // 2)
+        load_weight_columns(2, N_TILE // 2, N_TILE // 2)
         load_rows(3)
         load_weight_columns(N_TILES - 1)
         for i in range(4, ROW_TILES):
@@ -238,7 +241,8 @@ def tile_hopfieldmemorylayer_pa_kernel(tc, query_input, norm_query_w, W_in_words
         project(0, 1, passes=(0, 1))
         transpose(1, 1)
         project(0, 1, passes=(2, 3))
-        project(0, 2)
+        project(0, 2, 0, N_TILE // 2)
+        project(0, 2, N_TILE // 2, N_TILE // 2)
         gather(1, 0, "scalar")
         empty(0, 0, "scalar")
         gather(1, 1, "scalar")
@@ -248,7 +252,8 @@ def tile_hopfieldmemorylayer_pa_kernel(tc, query_input, norm_query_w, W_in_words
         quantise(1, 0, DUO)
         quantise(1, DUO, DUO)
         normalise(2, 1)
-        empty(0, 2, "scalar")
+        empty(0, 2, "scalar", 0, N_TILE // 2)
+        empty(0, 2, "scalar", N_TILE // 2, N_TILE // 2)
         statistics(3)
 
         project(1, 0)

@@ -27,6 +27,7 @@ SCALE_ROWS = 4
 QUADRANTS = 4
 DUO = 2
 DUOS = PASSES // DUO
+SIDES = 2
 QUARTERS = 4
 EPS = 1e-6
 
@@ -59,10 +60,11 @@ def tile_hopfieldmemorylayer_pa_kernel(tc, query_input, norm_query_w, W_in_words
         table_warm = keep.tile([P, 1], F32)
         squares_s = keep.tile([P, FEATURES], BF16)
         squares_v = keep.tile([P, FEATURES // QUARTERS], BF16)
-        first_sums = keep.tile([P, QUARTERS], F32)
-        first_copy = keep.tile([P, QUARTERS], F32)
+        piece_sums = keep.tile([P, ROW_TILES, QUARTERS], F32)
+        others = keep.tile([P, ROW_TILES], F32)
+        shift = keep.tile([P, ROW_TILES], F32)
         sum_squares = keep.tile([P, ROW_TILES], F32)
-        first_sum = keep.tile([P, 1], F32)
+        h_plain = keep.tile([P, FEATURES], BF16)
         rms = keep.tile([P, ROW_TILES], F32)
         inv_rms = keep.tile([P, ROW_TILES], F32)
         gain_banks = [gain_psum.tile([P, DUO * K_PASS], BF16, name="gain_bank%d" % b) for b in range(DUOS)]
@@ -83,12 +85,12 @@ def tile_hopfieldmemorylayer_pa_kernel(tc, query_input, norm_query_w, W_in_words
                     in_=W_in_scales[:, SCALE_ROWS * quadrant : SCALE_ROWS * (quadrant + 1), :].bitcast(I32),
                 )
 
-        def load_weight_columns(n, first=0, width=N_TILE):
+        def load_weights(g, side):
             words = W_in_words.rearrange("g p n t -> p g (n t)")
-            start = n * N_TILE + first
+            width = FEATURES // SIDES
             nc.sync.dma_start(
-                out=w_codes[:, :, start : start + width].bitcast(I32),
-                in_=words[:, :, start * PACK : (start + width) * PACK].bitcast(I32),
+                out=w_codes[:, g, side * width : (side + 1) * width].bitcast(I32),
+                in_=words[:, g, side * width * PACK : (side + 1) * width * PACK].bitcast(I32),
             )
 
         def spread_gain():
@@ -102,19 +104,31 @@ def tile_hopfieldmemorylayer_pa_kernel(tc, query_input, norm_query_w, W_in_words
                     stop=True,
                 )
 
-        def first_statistics():
-            width = FEATURES // QUARTERS
-            for q in range(QUARTERS):
-                piece = x_all[:, 0, q * width : (q + 1) * width]
-                if q >= QUARTERS // 2:
-                    nc.scalar.activation(out=squares_s[:, 0:width], in_=piece, func=ACT.Square, accum_out=first_sums[:, q : q + 1])
-                else:
-                    nc.vector.scalar_tensor_tensor(
-                        out=squares_v[:], in0=piece, scalar=1.0, in1=piece, op0=ALU.mult, op1=ALU.mult,
-                        accum_out=first_sums[:, q : q + 1],
-                    )
-            nc.scalar.activation(out=first_copy[:], in_=first_sums[:], func=ACT.Copy, accum_out=first_sum[:])
-            nc.scalar.activation(out=rms[:, 0:1], in_=first_sum[:], func=ACT.Sqrt, scale=1.0 / FEATURES, bias=eps[:])
+        def square(i, first, last, column):
+            nc.scalar.activation(
+                out=squares_s[:, 0 : last - first], in_=x_all[:, i, first:last], func=ACT.Square, accum_out=piece_sums[:, i, column : column + 1]
+            )
+
+        def square_on_vector(i, first, last, column):
+            piece = x_all[:, i, first:last]
+            nc.vector.scalar_tensor_tensor(
+                out=squares_v[:, 0 : last - first], in0=piece, scalar=1.0, in1=piece, op0=ALU.mult, op1=ALU.mult,
+                accum_out=piece_sums[:, i, column : column + 1],
+            )
+
+        def add_up(i, columns):
+            total = piece_sums[:, i, 0:1]
+            if columns > 2:
+                nc.vector.scalar_tensor_tensor(
+                    out=others[:, i : i + 1], in0=piece_sums[:, i, 0:1], scalar=0.0 if columns == 3 else piece_sums[:, i, 2:3],
+                    in1=piece_sums[:, i, 1:2], op0=ALU.add, op1=ALU.add,
+                )
+                total = others[:, i : i + 1]
+            nc.vector.tensor_scalar(out=shift[:, i : i + 1], in0=total, scalar1=1.0 / FEATURES, scalar2=EPS, op0=ALU.mult, op1=ALU.add)
+
+        def root(i, columns):
+            last = piece_sums[:, i, columns - 1 : columns]
+            nc.scalar.activation(out=rms[:, i : i + 1], in_=last, func=ACT.Sqrt, scale=1.0 / FEATURES, bias=shift[:, i : i + 1])
 
         def statistics(i):
             nc.scalar.activation(out=squares_s[:], in_=x_all[:, i, :], func=ACT.Square, accum_out=sum_squares[:, i : i + 1])
@@ -139,7 +153,25 @@ def tile_hopfieldmemorylayer_pa_kernel(tc, query_input, norm_query_w, W_in_words
                     op1=ALU.mult,
                 )
 
+        def normalise_first(g):
+            cols = slice(g * K_PASS, (g + 1) * K_PASS)
+            nc.vector.scalar_tensor_tensor(
+                out=h_plain[:, cols],
+                in0=x_all[:, 0, cols],
+                scalar=inv_rms[:, 0:1],
+                in1=gain_banks[g // DUO][:, (g % DUO) * K_PASS : (g % DUO + 1) * K_PASS],
+                op0=ALU.mult,
+                op1=ALU.mult,
+            )
+
         banks = {}
+
+        def transpose_first(g):
+            words = h_plain[:].bitcast(F32)
+            bank = turned.tile([P, DUO, HALVES, P], F32, name="bank")
+            for u in range(HALVES):
+                nc.tensor.transpose(bank[:, 0, u, :], words[:, g * HALVES * P + u : (g + 1) * HALVES * P : HALVES], identity[:])
+            banks[(0, g)] = bank
 
         def transpose(i, b):
             words = h_sorted[i][:].rearrange("r b u c e -> r (b u c e)").bitcast(F32)
@@ -151,6 +183,12 @@ def tile_hopfieldmemorylayer_pa_kernel(tc, query_input, norm_query_w, W_in_words
             banks[(i, b)] = bank
 
         h = {}
+
+        def gather_first(g):
+            if g == 0:
+                h[0] = work.tile([P, PASSES, P, PACK], BF16, align_bytes=64, name="h")
+            h_words = h[0][:].rearrange("p g r t -> p (g r t)").bitcast(F32).rearrange("p (g r u) -> p g r u", g=PASSES, u=HALVES)
+            nc.scalar.copy(out=h_words[:, g, :, :], in_=banks[(0, g)][:, 0, :, :].rearrange("p u r -> p r u"))
 
         def gather(i, b, engine):
             if i not in h:
@@ -206,74 +244,97 @@ def tile_hopfieldmemorylayer_pa_kernel(tc, query_input, norm_query_w, W_in_words
         load_first_rows()
         nc.sync.dma_start(out=gain_rows[0:PASSES, :], in_=norm_query_w.rearrange("(g j) -> g j", g=PASSES))
         load_rows(1)
-        load_rows(2)
         load_weight_scales()
-        load_weight_columns(0)
-        load_weight_columns(1)
-        load_weight_columns(2, 0, N_TILE // 2)
-        load_weight_columns(2, N_TILE // 2, N_TILE // 2)
+        load_weights(0, 0)
+        load_weights(1, 0)
+        load_rows(2)
+        load_weights(2, 0)
+        load_weights(3, 0)
+        load_weights(0, 1)
+        load_weights(1, 1)
         load_rows(3)
-        load_weight_columns(N_TILES - 1)
+        load_weights(2, 1)
+        load_weights(3, 1)
         for i in range(4, ROW_TILES):
             load_rows(i)
 
         spread_gain()
-        first_statistics()
+        square_on_vector(0, 0, 512, 0)
+        square(0, 512, 1024, 1)
+        square_on_vector(0, 1024, 1536, 2)
+        square(0, 1536, 2048, 3)
+        add_up(0, 4)
+        root(0, 4)
         invert(0)
-        statistics(1)
-        normalise(0, 0)
-        transpose(0, 0)
-        gather(0, 0, "scalar")
-        normalise(0, 1)
-        transpose(0, 1)
-        gather(0, 1, "scalar")
+        square(1, 0, 1024, 0)
+        normalise_first(0)
+        transpose_first(0)
+        square(1, 1024, 1536, 1)
+        gather_first(0)
+        normalise_first(1)
+        transpose_first(1)
+        gather_first(1)
+        square(1, 1536, 2048, 2)
+        normalise_first(2)
+        quantise(0, 0, 1)
+        transpose_first(2)
+        gather_first(2)
+        normalise_first(3)
+        quantise(0, 1, 1)
+        for n in (0, 1):
+            project(0, n, passes=(0,))
+        transpose_first(3)
+        gather_first(3)
+        add_up(1, 3)
+        root(1, 3)
+        quantise(0, 2, 1)
+        quantise(0, 3, 1)
         invert(1)
         normalise(1, 0, (0,))
-        quantise(0, 0, DUO)
         normalise(1, 0, (1,))
-        quantise(0, DUO, DUO)
         normalise(1, 1)
-        statistics(2)
-
-        project(0, 0, passes=(0, 1))
+        for g in (1, 2, 3):
+            for n in (0, 1):
+                project(0, n, passes=(g,))
         transpose(1, 0)
-        project(0, 0, passes=(2, 3))
-        project(0, 1, passes=(0, 1))
-        transpose(1, 1)
-        project(0, 1, passes=(2, 3))
-        project(0, 2, 0, N_TILE // 2)
-        project(0, 2, N_TILE // 2, N_TILE // 2)
+        statistics(2)
+        empty(0, 0, "vector")
+        empty(0, 1, "vector")
         gather(1, 0, "scalar")
-        empty(0, 0, "scalar")
+        transpose(1, 1)
         gather(1, 1, "scalar")
-        empty(0, 1, "scalar")
-        invert(2)
-        normalise(2, 0)
         quantise(1, 0, DUO)
+        invert(2)
         quantise(1, DUO, DUO)
+        normalise(2, 0)
         normalise(2, 1)
-        empty(0, 2, "scalar", 0, N_TILE // 2)
-        empty(0, 2, "scalar", N_TILE // 2, N_TILE // 2)
+        for g in (0, 1):
+            for n in (2, 3):
+                project(0, n, passes=(g,))
+        for n in (0, 1):
+            project(1, n, passes=(0, 1))
         statistics(3)
-
-        project(1, 0)
+        for n in (0, 1):
+            project(1, n, passes=(2, 3))
+        empty(1, 0, "vector")
+        empty(1, 1, "vector")
         transpose(2, 0)
+        gather(2, 0, "scalar")
+        for n in (2, 3):
+            project(0, n, passes=(2, 3))
         transpose(2, 1)
-        project(1, 1)
-        project(1, 2)
-        project(0, 3)
-        empty(1, 0, "scalar")
-        project(1, 3)
-        gather(2, 0, "vector")
-        gather(2, 1, "vector")
+        empty(0, 2, "scalar")
+        empty(0, 3, "scalar")
+        gather(2, 1, "scalar")
         invert(3)
         normalise(3, 0)
-        normalise(3, 1)
+        normalise(3, 1, (0,))
         quantise(2, 0, PASSES)
-        empty(1, 1, "scalar")
-        empty(1, 2, "scalar")
+        normalise(3, 1, (1,))
+        project(1, 2)
+        project(1, 3)
         statistics(4)
-        empty(0, 3, "scalar")
+        empty(1, 2, "scalar")
         left = (1, 3)
 
         for i in range(2, ROW_TILES - 1):

@@ -61,8 +61,7 @@ def tile_hopfieldmemorylayer_pa_kernel(tc, query_input, norm_query_w, W_in_words
         squares_s = keep.tile([P, FEATURES], BF16)
         squares_v = keep.tile([P, FEATURES // QUARTERS], BF16)
         piece_sums = keep.tile([P, ROW_TILES, QUARTERS], F32)
-        others = keep.tile([P, ROW_TILES], F32)
-        shift = keep.tile([P, ROW_TILES], F32)
+        piece_copy = keep.tile([P, QUARTERS], F32)
         sum_squares = keep.tile([P, ROW_TILES], F32)
         h_plain = keep.tile([P, FEATURES], BF16)
         rms = keep.tile([P, ROW_TILES], F32)
@@ -109,26 +108,16 @@ def tile_hopfieldmemorylayer_pa_kernel(tc, query_input, norm_query_w, W_in_words
                 out=squares_s[:, 0 : last - first], in_=x_all[:, i, first:last], func=ACT.Square, accum_out=piece_sums[:, i, column : column + 1]
             )
 
-        def square_on_vector(i, first, last, column):
-            piece = x_all[:, i, first:last]
+        def square_on_vector(first, last, column):
+            piece = x_all[:, 0, first:last]
             nc.vector.scalar_tensor_tensor(
                 out=squares_v[:, 0 : last - first], in0=piece, scalar=1.0, in1=piece, op0=ALU.mult, op1=ALU.mult,
-                accum_out=piece_sums[:, i, column : column + 1],
+                accum_out=piece_sums[:, 0, column : column + 1],
             )
 
-        def add_up(i, columns):
-            total = piece_sums[:, i, 0:1]
-            if columns > 2:
-                nc.vector.scalar_tensor_tensor(
-                    out=others[:, i : i + 1], in0=piece_sums[:, i, 0:1], scalar=0.0 if columns == 3 else piece_sums[:, i, 2:3],
-                    in1=piece_sums[:, i, 1:2], op0=ALU.add, op1=ALU.add,
-                )
-                total = others[:, i : i + 1]
-            nc.vector.tensor_scalar(out=shift[:, i : i + 1], in0=total, scalar1=1.0 / FEATURES, scalar2=EPS, op0=ALU.mult, op1=ALU.add)
-
         def root(i, columns):
-            last = piece_sums[:, i, columns - 1 : columns]
-            nc.scalar.activation(out=rms[:, i : i + 1], in_=last, func=ACT.Sqrt, scale=1.0 / FEATURES, bias=shift[:, i : i + 1])
+            nc.scalar.activation(out=piece_copy[:, 0:columns], in_=piece_sums[:, i, 0:columns], func=ACT.Copy, accum_out=sum_squares[:, i : i + 1])
+            nc.scalar.activation(out=rms[:, i : i + 1], in_=sum_squares[:, i : i + 1], func=ACT.Sqrt, scale=1.0 / FEATURES, bias=eps[:])
 
         def statistics(i):
             nc.scalar.activation(out=squares_s[:], in_=x_all[:, i, :], func=ACT.Square, accum_out=sum_squares[:, i : i + 1])
@@ -259,11 +248,10 @@ def tile_hopfieldmemorylayer_pa_kernel(tc, query_input, norm_query_w, W_in_words
             load_rows(i)
 
         spread_gain()
-        square_on_vector(0, 0, 512, 0)
+        square_on_vector(0, 512, 0)
         square(0, 512, 1024, 1)
-        square_on_vector(0, 1024, 1536, 2)
+        square_on_vector(1024, 1536, 2)
         square(0, 1536, 2048, 3)
-        add_up(0, 4)
         root(0, 4)
         invert(0)
         square(1, 0, 1024, 0)
@@ -285,7 +273,6 @@ def tile_hopfieldmemorylayer_pa_kernel(tc, query_input, norm_query_w, W_in_words
             project(0, n, passes=(0,))
         transpose_first(3)
         gather_first(3)
-        add_up(1, 3)
         root(1, 3)
         quantise(0, 2, 1)
         quantise(0, 3, 1)

@@ -29,6 +29,7 @@ DUO = 2
 DUOS = PASSES // DUO
 SIDES = 2
 QUARTERS = 4
+APART = 64
 EPS = 1e-6
 
 FLOPS = 2 * ROWS * FEATURES * FEATURES
@@ -49,8 +50,11 @@ def tile_hopfieldmemorylayer_pa_kernel(tc, query_input, norm_query_w, W_in_words
 
         x_all = keep.tile([P, ROW_TILES, FEATURES], BF16)
         w_codes = keep.tile([P, PASSES, FEATURES], U32, align_bytes=64)
+        apart_1 = keep.tile([P, APART], U8, align_bytes=64)
         w_planes = keep.tile([P, FEATURES], U8, align_bytes=64)
+        apart_2 = keep.tile([P, APART], U8, align_bytes=64)
         h_codes = keep.tile([P, ROW_TILES, PASSES, P], U32, align_bytes=64)
+        apart_3 = keep.tile([P, APART], U8, align_bytes=64)
         h_planes = keep.tile([P, ROW_TILES, PASSES, P], U8, align_bytes=64)
         result = keep.tile([P, ROW_TILES, FEATURES], F32)
         gain_rows = keep.tile([P, K_PASS], BF16)
@@ -226,6 +230,8 @@ def tile_hopfieldmemorylayer_pa_kernel(tc, query_input, norm_query_w, W_in_words
 
         nc.gpsimd.memset(gain_rows[:], 0.0)
         nc.vector.memset(w_planes[:].bitcast(I32), 0)
+        for gap in (apart_1, apart_2, apart_3):
+            nc.gpsimd.memset(gap[:], 0)
         nc.vector.memset(eps[:], EPS)
         nc.scalar.activation(out=table_warm[:], in_=eps[:], func=ACT.Sqrt)
         make_identity(nc, identity_bf[:])

from contextlib import ExitStack

import concourse.mybir as mybir
from concourse.masks import make_identity

F32 = mybir.dt.float32
BF16 = mybir.dt.bfloat16
U8 = mybir.dt.uint8
U32 = mybir.dt.uint32
I32 = mybir.dt.int32
FP8X4 = mybir.dt.float8_e4m3fn_x4
ACT = mybir.ActivationFunctionType
ALU = mybir.AluOpType

P = 128
PACK = 4
PAIR = 2
HALVES = PACK // PAIR
K_PASS = P * PACK
ROWS = 1024
FEATURES = 2048
PASSES = FEATURES // K_PASS
ROW_TILES = ROWS // P
N_TILE = 512
N_TILES = FEATURES // N_TILE
SCALE_ROWS = 4
QUADRANTS = 4
DUO = 2
DUOS = PASSES // DUO
SIDES = 2
QUARTERS = 4
APART = 64
EPS = 1e-6

FLOPS = 2 * ROWS * FEATURES * FEATURES


def tile_hopfieldmemorylayer_pa_kernel(tc, query_input, norm_query_w, W_in_words, W_in_scales, out):
    nc = tc.nc
    x_rows = query_input.flatten_outer_dims()
    out_rows = out.flatten_outer_dims()

    with ExitStack() as ctx:
        keep = ctx.enter_context(tc.tile_pool(name="keep", bufs=1))
        work = ctx.enter_context(tc.tile_pool(name="work", bufs=2))
        gain_psum = ctx.enter_context(tc.psum_pool(name="gain_psum", bufs=1))
        turned = ctx.enter_context(tc.psum_pool(name="turned", bufs=DUOS))
        sums = ctx.enter_context(tc.psum_pool(name="sums", bufs=N_TILES))
        ctx.enter_context(tc.manual_schedule())

        x_all = keep.tile([P, ROW_TILES, FEATURES], BF16)
        w_codes = keep.tile([P, PASSES, FEATURES], U32, align_bytes=64)
        apart_1 = keep.tile([P, APART], U8, align_bytes=64)
        w_planes = keep.tile([P, FEATURES], U8, align_bytes=64)
        apart_2 = keep.tile([P, APART], U8, align_bytes=64)
        h_codes = keep.tile([P, ROW_TILES, PASSES, P], U32, align_bytes=64)
        apart_3 = keep.tile([P, APART], U8, align_bytes=64)
        h_planes = keep.tile([P, ROW_TILES, PASSES, P], U8, align_bytes=64)
        result = keep.tile([P, ROW_TILES, FEATURES], F32)
        gain_rows = keep.tile([P, K_PASS], BF16)
        identity = keep.tile([P, P], F32)
        identity_bf = keep.tile([P, P], BF16)
        eps = keep.tile([P, 1], F32)
        table_warm = keep.tile([P, 1], F32)
        squares_s = keep.tile([P, FEATURES], BF16)
        squares_v = keep.tile([P, FEATURES // QUARTERS], BF16)
        piece_sums = keep.tile([P, ROW_TILES, QUARTERS], F32)
        piece_copy = keep.tile([P, QUARTERS], F32)
        sum_squares = keep.tile([P, ROW_TILES], F32)
        h_plain = keep.tile([P, FEATURES], BF16)
        rms = keep.tile([P, ROW_TILES], F32)
        inv_rms = keep.tile([P, ROW_TILES], F32)
        gain_banks = [gain_psum.tile([P, DUO * K_PASS], BF16, name="gain_bank%d" % b) for b in range(DUOS)]

        def load_rows(i):
            nc.sync.dma_start(out=x_all[:, i, :], in_=x_rows[i * P : (i + 1) * P, :])

        def load_first_rows():
            width = FEATURES // QUARTERS
            for q in range(QUARTERS):
                nc.sync.dma_start(out=x_all[:, 0, q * width : (q + 1) * width], in_=x_rows[0:P, q * width : (q + 1) * width])

        def load_weight_scales():
            for quadrant in range(QUADRANTS):
                first = 32 * quadrant
                nc.sync.dma_start(
                    out=w_planes[first : first + PASSES * SCALE_ROWS, :].bitcast(I32),
                    in_=W_in_scales[:, SCALE_ROWS * quadrant : SCALE_ROWS * (quadrant + 1), :].bitcast(I32),
                )

        def load_weights(g, side):
            words = W_in_words.rearrange("g p n t -> p g (n t)")
            width = FEATURES // SIDES
            nc.sync.dma_start(
                out=w_codes[:, g, side * width : (side + 1) * width].bitcast(I32),
                in_=words[:, g, side * width * PACK : (side + 1) * width * PACK].bitcast(I32),
            )

        def spread_gain():
            for g in range(PASSES):
                first = (g % DUO) * K_PASS
                nc.tensor.matmul(
                    out=gain_banks[g // DUO][:, first : first + K_PASS],
                    lhsT=identity_bf[:, g : g + 1].to_broadcast([P, P]),
                    rhs=gain_rows[:],
                    start=True,
                    stop=True,
                )

        def square(i, first, last, column):
            nc.scalar.activation(
                out=squares_s[:, 0 : last - first], in_=x_all[:, i, first:last], func=ACT.Square, accum_out=piece_sums[:, i, column : column + 1]
            )

        def square_on_vector(first, last, column):
            piece = x_all[:, 0, first:last]
            nc.vector.scalar_tensor_tensor(
                out=squares_v[:, 0 : last - first], in0=piece, scalar=1.0, in1=piece, op0=ALU.mult, op1=ALU.mult,
                accum_out=piece_sums[:, 0, column : column + 1],
            )

        def root(i, columns):
            nc.scalar.activation(out=piece_copy[:, 0:columns], in_=piece_sums[:, i, 0:columns], func=ACT.Copy, accum_out=sum_squares[:, i : i + 1])
            nc.scalar.activation(out=rms[:, i : i + 1], in_=sum_squares[:, i : i + 1], func=ACT.Sqrt, scale=1.0 / FEATURES, bias=eps[:])

        def statistics(i):
            nc.scalar.activation(out=squares_s[:], in_=x_all[:, i, :], func=ACT.Square, accum_out=sum_squares[:, i : i + 1])
            nc.scalar.activation(out=rms[:, i : i + 1], in_=sum_squares[:, i : i + 1], func=ACT.Sqrt, scale=1.0 / FEATURES, bias=eps[:])

        def invert(i):
            nc.vector.reciprocal(inv_rms[:, i : i + 1], rms[:, i : i + 1])

        h_sorted = {}

        def normalise(i, b, halves=(0, 1)):
            if i not in h_sorted:
                h_sorted[i] = work.tile([P, DUOS, HALVES, DUO * P, PAIR], BF16, name="h_sorted")
            pairs = x_all[:, i, b * DUO * K_PASS : (b + 1) * DUO * K_PASS].rearrange("r (c u e) -> r u c e", u=HALVES, e=PAIR)
            for u in halves:
                nc.vector.scalar_tensor_tensor(
                    out=h_sorted[i][:, b, u, :, :],
                    in0=pairs[:, u, :, :],
                    scalar=inv_rms[:, i : i + 1],
                    in1=gain_banks[b][:].rearrange("r (c u e) -> r u c e", u=HALVES, e=PAIR)[:, u, :, :],
                    op0=ALU.mult,
                    op1=ALU.mult,
                )

        def normalise_first(g):
            cols = slice(g * K_PASS, (g + 1) * K_PASS)
            nc.vector.scalar_tensor_tensor(
                out=h_plain[:, cols],
                in0=x_all[:, 0, cols],
                scalar=inv_rms[:, 0:1],
                in1=gain_banks[g // DUO][:, (g % DUO) * K_PASS : (g % DUO + 1) * K_PASS],
                op0=ALU.mult,
                op1=ALU.mult,
            )

        banks = {}

        def transpose_first(g):
            words = h_plain[:].bitcast(F32)
            bank = turned.tile([P, DUO, HALVES, P], F32, name="bank")
            for u in range(HALVES):
                nc.tensor.transpose(bank[:, 0, u, :], words[:, g * HALVES * P + u : (g + 1) * HALVES * P : HALVES], identity[:])
            banks[(0, g)] = bank

        def transpose(i, b):
            words = h_sorted[i][:].rearrange("r b u c e -> r (b u c e)").bitcast(F32)
            bank = turned.tile([P, DUO, HALVES, P], F32, name="bank")
            for u in range(HALVES):
                for j in range(DUO):
                    first = ((b * HALVES + u) * DUO + j) * P
                    nc.tensor.transpose(bank[:, j, u, :], words[:, first : first + P], identity[:])
            banks[(i, b)] = bank

        h = {}

        def gather_first(g):
            if g == 0:
                h[0] = work.tile([P, PASSES, P, PACK], BF16, align_bytes=64, name="h")
            h_words = h[0][:].rearrange("p g r t -> p (g r t)").bitcast(F32).rearrange("p (g r u) -> p g r u", g=PASSES, u=HALVES)
            nc.scalar.copy(out=h_words[:, g, :, :], in_=banks[(0, g)][:, 0, :, :].rearrange("p u r -> p r u"))

        def gather(i, b, engine):
            if i not in h:
                h[i] = work.tile([P, PASSES, P, PACK], BF16, align_bytes=64, name="h")
            h_words = h[i][:].rearrange("p g r t -> p (g r t)").bitcast(F32).rearrange("p (g r u) -> p g r u", g=PASSES, u=HALVES)
            dst = h_words[:, b * DUO : (b + 1) * DUO, :, :]
            src = banks[(i, b)][:].rearrange("p g u r -> p g r u")
            if engine == "scalar":
                nc.scalar.copy(out=dst, in_=src)
            else:
                nc.vector.tensor_copy(out=dst, in_=src)

        def quantise(i, first_pass, passes):
            chosen = slice(first_pass, first_pass + passes)
            nc.vector.quantize_mx(
                out=h_codes[:, i, chosen, :].rearrange("p g r -> p (g r)").bitcast(FP8X4),
                scales=h_planes[:, i, chosen, :].rearrange("p g r -> p (g r)"),
                in_=h[i][:, chosen, :, :].rearrange("p g r t -> p (g r t)"),
            )

        open_banks = {}

        def project(i, n, first=0, width=N_TILE, passes=(0, 1, 2, 3)):
            n_cols = slice(n * N_TILE + first, n * N_TILE + first + width)
            if passes[0] == 0:
                open_banks[(i, n, first)] = sums.tile([P, width], F32, name="acc")
            acc = open_banks[(i, n, first)]
            for g in passes:
                nc.tensor.matmul_mx(
                    out=acc[:],
                    lhsT=h_codes[:, i, g, :].bitcast(FP8X4),
                    lhsT_scale=h_planes[:, i, g, :],
                    rhs=w_codes[:, g, n_cols].bitcast(FP8X4),
                    rhs_scale=w_planes[SCALE_ROWS * g : P, n_cols],
                    start=(g == 0),
                    stop=(g == PASSES - 1),
                )

        def empty(i, n, engine, first=0, width=N_TILE):
            n_cols = slice(n * N_TILE + first, n * N_TILE + first + width)
            if engine == "scalar":
                nc.scalar.copy(out=result[:, i, n_cols], in_=open_banks[(i, n, first)][:])
            else:
                nc.vector.tensor_copy(out=result[:, i, n_cols], in_=open_banks[(i, n, first)][:])
            nc.sync.dma_start(out=out_rows[i * P : (i + 1) * P, n_cols], in_=result[:, i, n_cols])

        nc.gpsimd.memset(gain_rows[:], 0.0)
        nc.vector.memset(w_planes[:].bitcast(I32), 0)
        for gap in (apart_1, apart_2, apart_3):
            nc.gpsimd.memset(gap[:], 0)
        nc.vector.memset(eps[:], EPS)
        nc.scalar.activation(out=table_warm[:], in_=eps[:], func=ACT.Sqrt)
        make_identity(nc, identity_bf[:])
        make_identity(nc, identity[:])
        load_first_rows()
        nc.sync.dma_start(out=gain_rows[0:PASSES, :], in_=norm_query_w.rearrange("(g j) -> g j", g=PASSES))
        load_rows(1)
        load_weight_scales()
        load_weights(0, 0)
        load_weights(1, 0)
        load_rows(2)
        load_weights(2, 0)
        load_weights(3, 0)
        load_weights(0, 1)
        load_weights(1, 1)
        load_rows(3)
        load_weights(2, 1)
        load_weights(3, 1)
        for i in range(4, ROW_TILES):
            load_rows(i)

        spread_gain()
        square_on_vector(0, 512, 0)
        square(0, 512, 1024, 1)
        square_on_vector(1024, 1536, 2)
        square(0, 1536, 2048, 3)
        root(0, 4)
        invert(0)
        square(1, 0, 1024, 0)
        normalise_first(0)
        transpose_first(0)
        square(1, 1024, 1536, 1)
        gather_first(0)
        normalise_first(1)
        transpose_first(1)
        gather_first(1)
        square(1, 1536, 2048, 2)
        normalise_first(2)
        quantise(0, 0, 1)
        transpose_first(2)
        gather_first(2)
        normalise_first(3)
        quantise(0, 1, 1)
        for n in (0, 1):
            project(0, n, passes=(0,))
        transpose_first(3)
        gather_first(3)
        root(1, 3)
        quantise(0, 2, 1)
        quantise(0, 3, 1)
        invert(1)
        normalise(1, 0, (0,))
        normalise(1, 0, (1,))
        normalise(1, 1)
        for g in (1, 2, 3):
            for n in (0, 1):
                project(0, n, passes=(g,))
        transpose(1, 0)
        statistics(2)
        empty(0, 0, "vector")
        empty(0, 1, "vector")
        gather(1, 0, "scalar")
        transpose(1, 1)
        gather(1, 1, "scalar")
        quantise(1, 0, DUO)
        invert(2)
        quantise(1, DUO, DUO)
        normalise(2, 0)
        normalise(2, 1)
        for g in (0, 1):
            for n in (2, 3):
                project(0, n, passes=(g,))
        for n in (0, 1):
            project(1, n, passes=(0, 1))
        statistics(3)
        for n in (0, 1):
            project(1, n, passes=(2, 3))
        empty(1, 0, "vector")
        empty(1, 1, "vector")
        transpose(2, 0)
        gather(2, 0, "scalar")
        for n in (2, 3):
            project(0, n, passes=(2, 3))
        transpose(2, 1)
        empty(0, 2, "scalar")
        empty(0, 3, "scalar")
        gather(2, 1, "scalar")
        invert(3)
        normalise(3, 0)
        normalise(3, 1, (0,))
        quantise(2, 0, PASSES)
        normalise(3, 1, (1,))
        project(1, 2)
        project(1, 3)
        statistics(4)
        empty(1, 2, "scalar")
        left = (1, 3)

        for i in range(2, ROW_TILES - 1):
            if i + 1 < ROW_TILES:
                transpose(i + 1, 0)
                transpose(i + 1, 1)
            empty(left[0], left[1], "vector")
            left = (i, N_TILES - 1)
            for n in range(N_TILES):
                project(i, n)
            if i + 1 < ROW_TILES:
                gather(i + 1, 0, "vector")
                gather(i + 1, 1, "vector")
            if i + 2 < ROW_TILES:
                invert(i + 2)
                normalise(i + 2, 0)
                normalise(i + 2, 1)
            if i + 1 < ROW_TILES:
                quantise(i + 1, 0, PASSES)
            if i + 3 < ROW_TILES:
                statistics(i + 3)
            for n in range(N_TILES - 1):
                empty(i, n, "scalar")

        i = ROW_TILES - 1
        half = N_TILE // 2
        empty(left[0], left[1], "vector")
        for n in range(N_TILES - 1):
            project(i, n)
        project(i, N_TILES - 1, 0, half)
        empty(i, 0, "scalar")
        project(i, N_TILES - 1, half, half)
        empty(i, 1, "vector")
        empty(i, 2, "scalar")
        empty(i, N_TILES - 1, "vector", 0, half)
        empty(i, N_TILES - 1, "scalar", half, half)
